import numpy as np
import ml_dtypes

BF16 = ml_dtypes.bfloat16


def bf(x):
    return np.asarray(x, np.float32).astype(BF16)


def f32(x):
    return np.asarray(x, np.float32)


def f64(x):
    return np.asarray(x).astype(np.float64)


def striped(idx):
    return np.tile(idx.reshape(-1, 16).T, (8, 1))


C, S, NB, RB, N, H, K = 256, 1024, 4, 128, 4096, 512, 8
CUTOFF = 5.0


def swish(v):
    return v / (1.0 + np.exp(-v))


def setup_inputs():
    return {
        "x": f32(np.random.standard_normal((C, S))),
        "dw": bf(np.random.standard_normal((C, C)) / np.sqrt(C)),
        "db": f32(0.1 * np.random.standard_normal((C, 1))),
        "rbf": bf(np.random.standard_normal((RB, N))),
        "filt_w": bf(np.random.standard_normal((RB, C)) / np.sqrt(RB)),
        "dist": f32(0.9 * CUTOFF * np.random.random_sample((1, N))),
        "offs": striped(np.concatenate([np.random.permutation(S)[:H] for _ in range(K)])),
    }


def reference(x, dw, db, rbf, filt_w, dist, offs):
    idx = offs[:16].T.reshape(-1)
    xj = f64(dw).T @ swish(f64(x)) + f64(db)
    d = f64(dist) / CUTOFF
    cut = np.exp(1.0 - 1.0 / (1.0 - d * d))
    filt = (f64(filt_w).T @ f64(rbf)) * cut
    return (xj[:, idx] * filt).reshape(C, S, NB).sum(axis=2)

@@ -1,0 +1,114 @@
+import concourse.mybir as mybir
+
+F32 = mybir.dt.float32
+BF16 = mybir.dt.bfloat16
+U16 = mybir.dt.uint16
+ACT = mybir.ActivationFunctionType
+ALU = mybir.AluOpType
+AXIS = mybir.AxisListType
+
+P = 128
+C, S, NB, RB, N = 256, 1024, 4, 128, 4096
+CUTOFF = 5.0
+BLOCKS = C // P
+HALF = 512
+PIECE = 512
+PIECES = N // PIECE
+ATOMS = PIECE // NB
+PARK_ROWS = N // S
+
+FLOPS = 2 * C * C * S + 2 * RB * C * N
+
+
+def tile_physnetinteraction_kernel(tc, x, dw, db, rbf, filt_w, dist, offs, out):
+    nc = tc.nc
+    with (
+        tc.tile_pool(name="held", bufs=1) as held,
+        tc.tile_pool(name="ring", bufs=4) as ring,
+        tc.psum_pool(name="psum", bufs=2) as psum,
+    ):
+        dist_sb = held.tile([P, N // P], F32, name="dist_sb")
+        nc.sync.dma_start(dist_sb[:], dist.rearrange("o (p i) -> (o p) i", p=P))
+        offsets = held.tile([P, N // 16], U16, name="offsets")
+        nc.sync.dma_start(offsets[:], offs)
+
+        x_sb = [held.tile([P, S], F32, name=f"x_sb{kb}") for kb in range(BLOCKS)]
+        for h in range(S // HALF):
+            for kb in range(BLOCKS):
+                nc.sync.dma_start(
+                    x_sb[kb][:, h * HALF : (h + 1) * HALF],
+                    x[kb * P : (kb + 1) * P, h * HALF : (h + 1) * HALF],
+                )
+        rbf_sb = held.tile([RB, N], BF16, name="rbf_sb")
+        for h in range(2):
+            nc.sync.dma_start(rbf_sb[:, h * (N // 2) : (h + 1) * (N // 2)], rbf[:, h * (N // 2) : (h + 1) * (N // 2)])
+
+        dw_sb = [held.tile([P, C], BF16, name=f"dw_sb{kb}") for kb in range(BLOCKS)]
+        db_sb = [held.tile([P, 1], F32, name=f"db_sb{cb}") for cb in range(BLOCKS)]
+        for b in range(BLOCKS):
+            nc.scalar.dma_start(dw_sb[b][:], dw[b * P : (b + 1) * P, :])
+        for b in range(BLOCKS):
+            nc.scalar.dma_start(db_sb[b][:], db[b * P : (b + 1) * P, :])
+        fw_sb = held.tile([RB, C], BF16, name="fw_sb")
+        nc.scalar.dma_start(fw_sb[:], filt_w)
+
+        d2 = held.tile([P, N // P], F32, name="d2")
+        nc.scalar.activation(d2[:], dist_sb[:], ACT.Square, scale=1.0 / CUTOFF)
+        one_minus = held.tile([P, N // P], F32, name="one_minus")
+        nc.vector.tensor_scalar(one_minus[:], d2[:], -1.0, 1.0, ALU.mult, ALU.add)
+        recip = held.tile([P, N // P], F32, name="recip")
+        nc.vector.reciprocal(recip[:], one_minus[:])
+        cut = held.tile([P, N // P], F32, name="cut")
+        nc.scalar.activation(cut[:], recip[:], ACT.Exp, bias=1.0, scale=-1.0)
+
+        nc.sync.dma_start(out[0:PARK_ROWS, :].rearrange("r (q i) -> (r q) i", i=N // P), cut[:])
+        cut_all = held.tile([P, N], F32, name="cut_all")
+        for r in range(PARK_ROWS):
+            nc.sync.dma_start(cut_all[:, r * S : (r + 1) * S], out[r : r + 1, :].broadcast_to([P, S]))
+
+        sw = [held.tile([P, S], BF16, name=f"sw{kb}") for kb in range(BLOCKS)]
+        for h in range(S // HALF):
+            for kb in range(BLOCKS):
+                cols = slice(h * HALF, (h + 1) * HALF)
+                nc.scalar.activation(sw[kb][:, cols], x_sb[kb][:, cols], ACT.Silu)
+        xj = [held.tile([P, S], F32, name=f"xj{cb}") for cb in range(BLOCKS)]
+        for cb in range(BLOCKS):
+            for h in range(S // HALF):
+                cols = slice(h * HALF, (h + 1) * HALF)
+                xj_ps = psum.tile([P, HALF], F32, name="xj_ps")
+                for kb in range(BLOCKS):
+                    nc.tensor.matmul(
+                        xj_ps[:],
+                        dw_sb[kb][:, cb * P : (cb + 1) * P],
+                        sw[kb][:, cols],
+                        start=(kb == 0),
+                        stop=(kb == BLOCKS - 1),
+                    )
+                nc.scalar.activation(xj[cb][:, cols], xj_ps[:], ACT.Identity, bias=db_sb[cb][:, 0:1])
+
+        fw32 = held.tile([RB, C], F32, name="fw32")
+        nc.gpsimd.tensor_copy(fw32[:], fw_sb[:])
+        rbf_cut = held.tile([RB, N], F32, name="rbf_cut")
+        out_sb = [held.tile([P, S], F32, name=f"out_sb{cb}") for cb in range(BLOCKS)]
+        for k in range(PIECES):
+            pairs = slice(k * PIECE, (k + 1) * PIECE)
+            atoms = slice(k * ATOMS, (k + 1) * ATOMS)
+            nc.gpsimd.tensor_tensor(rbf_cut[:, pairs], rbf_sb[:, pairs], cut_all[:, pairs], ALU.mult)
+            for cb in range(BLOCKS):
+                filt_ps = psum.tile([P, PIECE], F32, name="filt_ps", bufs=4)
+                nc.tensor.matmul(filt_ps[:], fw32[:, cb * P : (cb + 1) * P], rbf_cut[:, pairs], start=True, stop=True)
+                filt = ring.tile([P, PIECE], F32, name="filt")
+                nc.scalar.copy(filt[:], filt_ps[:])
+                prod = ring.tile([P, PIECE], F32, name="prod")
+                nc.vector.tensor_tensor(
+                    prod[:],
+                    xj[cb][:].indirect(offsets[:, k * (PIECE // 16) : (k + 1) * (PIECE // 16)]),
+                    filt[:],
+                    ALU.mult,
+                )
+                nc.vector.tensor_reduce(
+                    out_sb[cb][:, atoms], prod[:].rearrange("p (a n) -> p a n", n=NB), axis=AXIS.X, op=ALU.add
+                )
+                if k % 2 == 1:
+                    done = slice((k - 1) * ATOMS, (k + 1) * ATOMS)
+                    nc.sync.dma_start(out[cb * P : (cb + 1) * P, done], out_sb[cb][:, done])

@@ -29,48 +29,46 @@ def tile_physnetinteraction_kernel(tc, x, dw, db, rbf, filt_w, dist, offs, out):
     ):
         dist_sb = held.tile([P, N // P], F32, name="dist_sb")
         nc.sync.dma_start(dist_sb[:], dist.rearrange("o (p i) -> (o p) i", p=P))
+        x_sb = held.tile([P, BLOCKS, S], F32, name="x_sb")
+        x_blocks = x.rearrange("(kb p) s -> p kb s", p=P)
+        for h in range(S // HALF):
+            cols = slice(h * HALF, (h + 1) * HALF)
+            nc.sync.dma_start(x_sb[:, :, cols], x_blocks[:, :, cols])
+        rbf_sb = held.tile([RB, N], BF16, name="rbf_sb")
+        for h in range(2):
+            cols = slice(h * (N // 2), (h + 1) * (N // 2))
+            nc.sync.dma_start(rbf_sb[:, cols], rbf[:, cols])
         offsets = held.tile([P, N // 16], U16, name="offsets")
         nc.sync.dma_start(offsets[:], offs)
 
-        x_sb = [held.tile([P, S], F32, name=f"x_sb{kb}") for kb in range(BLOCKS)]
-        for h in range(S // HALF):
-            for kb in range(BLOCKS):
-                nc.sync.dma_start(
-                    x_sb[kb][:, h * HALF : (h + 1) * HALF],
-                    x[kb * P : (kb + 1) * P, h * HALF : (h + 1) * HALF],
-                )
-        rbf_sb = held.tile([RB, N], BF16, name="rbf_sb")
-        for h in range(2):
-            nc.sync.dma_start(rbf_sb[:, h * (N // 2) : (h + 1) * (N // 2)], rbf[:, h * (N // 2) : (h + 1) * (N // 2)])
-
-        dw_sb = [held.tile([P, C], BF16, name=f"dw_sb{kb}") for kb in range(BLOCKS)]
+        dw_sb = held.tile([P, BLOCKS, C], BF16, name="dw_sb")
+        nc.gpsimd.dma_start(dw_sb[:], dw.rearrange("(kb p) c -> p kb c", p=P))
         db_sb = [held.tile([P, 1], F32, name=f"db_sb{cb}") for cb in range(BLOCKS)]
-        for b in range(BLOCKS):
-            nc.scalar.dma_start(dw_sb[b][:], dw[b * P : (b + 1) * P, :])
-        for b in range(BLOCKS):
-            nc.scalar.dma_start(db_sb[b][:], db[b * P : (b + 1) * P, :])
+        for cb in range(BLOCKS):
+            nc.gpsimd.dma_start(db_sb[cb][:], db[cb * P : (cb + 1) * P, :])
         fw_sb = held.tile([RB, C], BF16, name="fw_sb")
-        nc.scalar.dma_start(fw_sb[:], filt_w)
+        nc.gpsimd.dma_start(fw_sb[:], filt_w)
 
         d2 = held.tile([P, N // P], F32, name="d2")
-        nc.scalar.activation(d2[:], dist_sb[:], ACT.Square, scale=1.0 / CUTOFF)
+        nc.vector.tensor_tensor(d2[:], dist_sb[:], dist_sb[:], ALU.mult)
         one_minus = held.tile([P, N // P], F32, name="one_minus")
-        nc.vector.tensor_scalar(one_minus[:], d2[:], -1.0, 1.0, ALU.mult, ALU.add)
+        nc.vector.tensor_scalar(one_minus[:], d2[:], -1.0 / (CUTOFF * CUTOFF), 1.0, ALU.mult, ALU.add)
         recip = held.tile([P, N // P], F32, name="recip")
         nc.vector.reciprocal(recip[:], one_minus[:])
         cut = held.tile([P, N // P], F32, name="cut")
         nc.scalar.activation(cut[:], recip[:], ACT.Exp, bias=1.0, scale=-1.0)
 
         nc.sync.dma_start(out[0:PARK_ROWS, :].rearrange("r (q i) -> (r q) i", i=N // P), cut[:])
+        parked = out[0:PARK_ROWS, :].rearrange("r (h j) -> (r h) j", j=PIECE)
         cut_all = held.tile([P, N], F32, name="cut_all")
-        for r in range(PARK_ROWS):
-            nc.sync.dma_start(cut_all[:, r * S : (r + 1) * S], out[r : r + 1, :].broadcast_to([P, S]))
+        for k in range(PIECES):
+            nc.sync.dma_start(cut_all[:, k * PIECE : (k + 1) * PIECE], parked[k : k + 1, :].broadcast_to([P, PIECE]))
 
-        sw = [held.tile([P, S], BF16, name=f"sw{kb}") for kb in range(BLOCKS)]
+        sw = held.tile([P, BLOCKS, S], BF16, name="sw")
         for h in range(S // HALF):
             for kb in range(BLOCKS):
                 cols = slice(h * HALF, (h + 1) * HALF)
-                nc.scalar.activation(sw[kb][:, cols], x_sb[kb][:, cols], ACT.Silu)
+                nc.scalar.activation(sw[:, kb, cols], x_sb[:, kb, cols], ACT.Silu)
         xj = [held.tile([P, S], F32, name=f"xj{cb}") for cb in range(BLOCKS)]
         for cb in range(BLOCKS):
             for h in range(S // HALF):
@@ -79,8 +77,8 @@ def tile_physnetinteraction_kernel(tc, x, dw, db, rbf, filt_w, dist, offs, out):
                 for kb in range(BLOCKS):
                     nc.tensor.matmul(
                         xj_ps[:],
-                        dw_sb[kb][:, cb * P : (cb + 1) * P],
-                        sw[kb][:, cols],
+                        dw_sb[:, kb, cb * P : (cb + 1) * P],
+                        sw[:, kb, cols],
                         start=(kb == 0),
                         stop=(kb == BLOCKS - 1),
                     )
@@ -89,11 +87,14 @@ def tile_physnetinteraction_kernel(tc, x, dw, db, rbf, filt_w, dist, offs, out):
         fw32 = held.tile([RB, C], F32, name="fw32")
         nc.gpsimd.tensor_copy(fw32[:], fw_sb[:])
         rbf_cut = held.tile([RB, N], F32, name="rbf_cut")
+        for k in range(PIECES):
+            pairs = slice(k * PIECE, (k + 1) * PIECE)
+            nc.vector.tensor_tensor(rbf_cut[:, pairs], rbf_sb[:, pairs], cut_all[:, pairs], ALU.mult)
+
         out_sb = [held.tile([P, S], F32, name=f"out_sb{cb}") for cb in range(BLOCKS)]
         for k in range(PIECES):
             pairs = slice(k * PIECE, (k + 1) * PIECE)
             atoms = slice(k * ATOMS, (k + 1) * ATOMS)
-            nc.gpsimd.tensor_tensor(rbf_cut[:, pairs], rbf_sb[:, pairs], cut_all[:, pairs], ALU.mult)
             for cb in range(BLOCKS):
                 filt_ps = psum.tile([P, PIECE], F32, name="filt_ps", bufs=4)
                 nc.tensor.matmul(filt_ps[:], fw32[:, cb * P : (cb + 1) * P], rbf_cut[:, pairs], start=True, stop=True)

@@ -5,7 +5,6 @@ BF16 = mybir.dt.bfloat16
 U16 = mybir.dt.uint16
 ACT = mybir.ActivationFunctionType
 ALU = mybir.AluOpType
-AXIS = mybir.AxisListType
 
 P = 128
 C, S, NB, RB, N = 256, 1024, 4, 128, 4096
@@ -15,6 +14,7 @@ HALF = 512
 PIECE = 512
 PIECES = N // PIECE
 ATOMS = PIECE // NB
+GROUP = 2
 PARK_ROWS = N // S
 
 FLOPS = 2 * C * C * S + 2 * RB * C * N
@@ -92,24 +92,30 @@ def tile_physnetinteraction_kernel(tc, x, dw, db, rbf, filt_w, dist, offs, out):
             nc.vector.tensor_tensor(rbf_cut[:, pairs], rbf_sb[:, pairs], cut_all[:, pairs], ALU.mult)
 
         out_sb = [held.tile([P, S], F32, name=f"out_sb{cb}") for cb in range(BLOCKS)]
-        for k in range(PIECES):
-            pairs = slice(k * PIECE, (k + 1) * PIECE)
-            atoms = slice(k * ATOMS, (k + 1) * ATOMS)
+        for g in range(PIECES // GROUP):
+            atoms = slice(g * GROUP * ATOMS, (g + 1) * GROUP * ATOMS)
             for cb in range(BLOCKS):
-                filt_ps = psum.tile([P, PIECE], F32, name="filt_ps", bufs=4)
-                nc.tensor.matmul(filt_ps[:], fw32[:, cb * P : (cb + 1) * P], rbf_cut[:, pairs], start=True, stop=True)
-                filt = ring.tile([P, PIECE], F32, name="filt")
-                nc.scalar.copy(filt[:], filt_ps[:])
-                prod = ring.tile([P, PIECE], F32, name="prod")
-                nc.vector.tensor_tensor(
-                    prod[:],
-                    xj[cb][:].indirect(offsets[:, k * (PIECE // 16) : (k + 1) * (PIECE // 16)]),
-                    filt[:],
-                    ALU.mult,
+                prod = ring.tile([P, GROUP * PIECE], F32, name="prod")
+                for i in range(GROUP):
+                    k = g * GROUP + i
+                    pairs = slice(k * PIECE, (k + 1) * PIECE)
+                    filt_ps = psum.tile([P, PIECE], F32, name="filt_ps", bufs=4)
+                    nc.tensor.matmul(
+                        filt_ps[:], fw32[:, cb * P : (cb + 1) * P], rbf_cut[:, pairs], start=True, stop=True
+                    )
+                    filt = ring.tile([P, PIECE], F32, name="filt")
+                    nc.scalar.copy(filt[:], filt_ps[:])
+                    nc.vector.tensor_tensor(
+                        prod[:, i * PIECE : (i + 1) * PIECE],
+                        xj[cb][:].indirect(offsets[:, k * (PIECE // 16) : (k + 1) * (PIECE // 16)]),
+                        filt[:],
+                        ALU.mult,
+                    )
+                by_two = prod[:].rearrange("p (a m n) -> p m a n", m=2, n=2)
+                pair_sum = ring.tile([P, GROUP * PIECE // 2], F32, name="pair_sum")
+                nc.gpsimd.tensor_tensor(
+                    pair_sum[:].rearrange("p (a n) -> p a n", n=2), by_two[:, 0], by_two[:, 1], ALU.add
                 )
-                nc.vector.tensor_reduce(
-                    out_sb[cb][:, atoms], prod[:].rearrange("p (a n) -> p a n", n=NB), axis=AXIS.X, op=ALU.add
-                )
-                if k % 2 == 1:
-                    done = slice((k - 1) * ATOMS, (k + 1) * ATOMS)
-                    nc.sync.dma_start(out[cb * P : (cb + 1) * P, done], out_sb[cb][:, done])
+                by_one = pair_sum[:].rearrange("p (a n) -> p n a", n=2)
+                nc.gpsimd.tensor_tensor(out_sb[cb][:, atoms], by_one[:, 0], by_one[:, 1], ALU.add)
+                nc.sync.dma_start(out[cb * P : (cb + 1) * P, atoms], out_sb[cb][:, atoms])

@@ -113,9 +113,9 @@ def tile_physnetinteraction_kernel(tc, x, dw, db, rbf, filt_w, dist, offs, out):
                     )
                 by_two = prod[:].rearrange("p (a m n) -> p m a n", m=2, n=2)
                 pair_sum = ring.tile([P, GROUP * PIECE // 2], F32, name="pair_sum")
-                nc.gpsimd.tensor_tensor(
+                nc.vector.tensor_tensor(
                     pair_sum[:].rearrange("p (a n) -> p a n", n=2), by_two[:, 0], by_two[:, 1], ALU.add
                 )
                 by_one = pair_sum[:].rearrange("p (a n) -> p n a", n=2)
-                nc.gpsimd.tensor_tensor(out_sb[cb][:, atoms], by_one[:, 0], by_one[:, 1], ALU.add)
+                nc.vector.tensor_tensor(out_sb[cb][:, atoms], by_one[:, 0], by_one[:, 1], ALU.add)
                 nc.sync.dma_start(out[cb * P : (cb + 1) * P, atoms], out_sb[cb][:, atoms])

@@ -69,8 +69,15 @@ def tile_physnetinteraction_kernel(tc, x, dw, db, rbf, filt_w, dist, offs, out):
             for kb in range(BLOCKS):
                 cols = slice(h * HALF, (h + 1) * HALF)
                 nc.scalar.activation(sw[:, kb, cols], x_sb[:, kb, cols], ACT.Silu)
-        xj = [held.tile([P, S], F32, name=f"xj{cb}") for cb in range(BLOCKS)]
+        fw32 = held.tile([RB, C], F32, name="fw32")
+        nc.gpsimd.tensor_copy(fw32[:], fw_sb[:])
+        rbf_cut = held.tile([RB, N], F32, name="rbf_cut")
+        for k in range(PIECES):
+            pairs = slice(k * PIECE, (k + 1) * PIECE)
+            nc.vector.tensor_tensor(rbf_cut[:, pairs], rbf_sb[:, pairs], cut_all[:, pairs], ALU.mult)
+
         for cb in range(BLOCKS):
+            xj = held.tile([P, S], F32, name=f"xj{cb}")
             for h in range(S // HALF):
                 cols = slice(h * HALF, (h + 1) * HALF)
                 xj_ps = psum.tile([P, HALF], F32, name="xj_ps")
@@ -82,40 +89,35 @@ def tile_physnetinteraction_kernel(tc, x, dw, db, rbf, filt_w, dist, offs, out):
                         start=(kb == 0),
                         stop=(kb == BLOCKS - 1),
                     )
-                nc.scalar.activation(xj[cb][:, cols], xj_ps[:], ACT.Identity, bias=db_sb[cb][:, 0:1])
+                nc.scalar.activation(xj[:, cols], xj_ps[:], ACT.Identity, bias=db_sb[cb][:, 0:1])
 
-        fw32 = held.tile([RB, C], F32, name="fw32")
-        nc.gpsimd.tensor_copy(fw32[:], fw_sb[:])
-        rbf_cut = held.tile([RB, N], F32, name="rbf_cut")
-        for k in range(PIECES):
-            pairs = slice(k * PIECE, (k + 1) * PIECE)
-            nc.vector.tensor_tensor(rbf_cut[:, pairs], rbf_sb[:, pairs], cut_all[:, pairs], ALU.mult)
-
-        out_sb = [held.tile([P, S], F32, name=f"out_sb{cb}") for cb in range(BLOCKS)]
-        for g in range(PIECES // GROUP):
-            atoms = slice(g * GROUP * ATOMS, (g + 1) * GROUP * ATOMS)
-            for cb in range(BLOCKS):
-                prod = ring.tile([P, GROUP * PIECE], F32, name="prod")
+            out_sb = held.tile([P, S], F32, name=f"out_sb{cb}")
+            for g in range(PIECES // GROUP):
+                atoms = slice(g * GROUP * ATOMS, (g + 1) * GROUP * ATOMS)
+                filt = ring.tile([P, GROUP * PIECE], F32, name="filt")
                 for i in range(GROUP):
                     k = g * GROUP + i
-                    pairs = slice(k * PIECE, (k + 1) * PIECE)
                     filt_ps = psum.tile([P, PIECE], F32, name="filt_ps", bufs=4)
                     nc.tensor.matmul(
-                        filt_ps[:], fw32[:, cb * P : (cb + 1) * P], rbf_cut[:, pairs], start=True, stop=True
+                        filt_ps[:],
+                        fw32[:, cb * P : (cb + 1) * P],
+                        rbf_cut[:, k * PIECE : (k + 1) * PIECE],
+                        start=True,
+                        stop=True,
                     )
-                    filt = ring.tile([P, PIECE], F32, name="filt")
-                    nc.scalar.copy(filt[:], filt_ps[:])
-                    nc.vector.tensor_tensor(
-                        prod[:, i * PIECE : (i + 1) * PIECE],
-                        xj[cb][:].indirect(offsets[:, k * (PIECE // 16) : (k + 1) * (PIECE // 16)]),
-                        filt[:],
-                        ALU.mult,
-                    )
+                    nc.scalar.copy(filt[:, i * PIECE : (i + 1) * PIECE], filt_ps[:])
+                prod = ring.tile([P, GROUP * PIECE], F32, name="prod")
+                nc.vector.tensor_tensor(
+                    prod[:],
+                    xj[:].indirect(offsets[:, g * (GROUP * PIECE // 16) : (g + 1) * (GROUP * PIECE // 16)]),
+                    filt[:],
+                    ALU.mult,
+                )
                 by_two = prod[:].rearrange("p (a m n) -> p m a n", m=2, n=2)
                 pair_sum = ring.tile([P, GROUP * PIECE // 2], F32, name="pair_sum")
                 nc.vector.tensor_tensor(
                     pair_sum[:].rearrange("p (a n) -> p a n", n=2), by_two[:, 0], by_two[:, 1], ALU.add
                 )
                 by_one = pair_sum[:].rearrange("p (a n) -> p n a", n=2)
-                nc.vector.tensor_tensor(out_sb[cb][:, atoms], by_one[:, 0], by_one[:, 1], ALU.add)
-                nc.sync.dma_start(out[cb * P : (cb + 1) * P, atoms], out_sb[cb][:, atoms])
+                nc.vector.tensor_tensor(out_sb[:, atoms], by_one[:, 0], by_one[:, 1], ALU.add)
+                nc.sync.dma_start(out[cb * P : (cb + 1) * P, atoms], out_sb[:, atoms])

@@ -76,8 +76,8 @@ def tile_physnetinteraction_kernel(tc, x, dw, db, rbf, filt_w, dist, offs, out):
             pairs = slice(k * PIECE, (k + 1) * PIECE)
             nc.vector.tensor_tensor(rbf_cut[:, pairs], rbf_sb[:, pairs], cut_all[:, pairs], ALU.mult)
 
+        xj = [held.tile([P, S], F32, name=f"xj{cb}") for cb in range(BLOCKS)]
         for cb in range(BLOCKS):
-            xj = held.tile([P, S], F32, name=f"xj{cb}")
             for h in range(S // HALF):
                 cols = slice(h * HALF, (h + 1) * HALF)
                 xj_ps = psum.tile([P, HALF], F32, name="xj_ps")
@@ -89,35 +89,53 @@ def tile_physnetinteraction_kernel(tc, x, dw, db, rbf, filt_w, dist, offs, out):
                         start=(kb == 0),
                         stop=(kb == BLOCKS - 1),
                     )
-                nc.scalar.activation(xj[:, cols], xj_ps[:], ACT.Identity, bias=db_sb[cb][:, 0:1])
+                nc.scalar.activation(xj[cb][:, cols], xj_ps[:], ACT.Identity, bias=db_sb[cb][:, 0:1])
 
-            out_sb = held.tile([P, S], F32, name=f"out_sb{cb}")
-            for g in range(PIECES // GROUP):
-                atoms = slice(g * GROUP * ATOMS, (g + 1) * GROUP * ATOMS)
-                filt = ring.tile([P, GROUP * PIECE], F32, name="filt")
-                for i in range(GROUP):
-                    k = g * GROUP + i
-                    filt_ps = psum.tile([P, PIECE], F32, name="filt_ps", bufs=4)
-                    nc.tensor.matmul(
-                        filt_ps[:],
-                        fw32[:, cb * P : (cb + 1) * P],
-                        rbf_cut[:, k * PIECE : (k + 1) * PIECE],
-                        start=True,
-                        stop=True,
-                    )
-                    nc.scalar.copy(filt[:, i * PIECE : (i + 1) * PIECE], filt_ps[:])
-                prod = ring.tile([P, GROUP * PIECE], F32, name="prod")
-                nc.vector.tensor_tensor(
-                    prod[:],
-                    xj[:].indirect(offsets[:, g * (GROUP * PIECE // 16) : (g + 1) * (GROUP * PIECE // 16)]),
-                    filt[:],
-                    ALU.mult,
+        out_sb = [held.tile([P, S], F32, name=f"out_sb{cb}") for cb in range(BLOCKS)]
+        units = [(cb, g) for cb in range(BLOCKS) for g in range(PIECES // GROUP)]
+        prods = {}
+        pair_sums = {}
+
+        def look_up(u):
+            cb, g = units[u]
+            filt = ring.tile([P, GROUP * PIECE], F32, name="filt")
+            for i in range(GROUP):
+                k = g * GROUP + i
+                filt_ps = psum.tile([P, PIECE], F32, name="filt_ps", bufs=4)
+                nc.tensor.matmul(
+                    filt_ps[:],
+                    fw32[:, cb * P : (cb + 1) * P],
+                    rbf_cut[:, k * PIECE : (k + 1) * PIECE],
+                    start=True,
+                    stop=True,
                 )
-                by_two = prod[:].rearrange("p (a m n) -> p m a n", m=2, n=2)
-                pair_sum = ring.tile([P, GROUP * PIECE // 2], F32, name="pair_sum")
-                nc.vector.tensor_tensor(
-                    pair_sum[:].rearrange("p (a n) -> p a n", n=2), by_two[:, 0], by_two[:, 1], ALU.add
-                )
-                by_one = pair_sum[:].rearrange("p (a n) -> p n a", n=2)
-                nc.vector.tensor_tensor(out_sb[:, atoms], by_one[:, 0], by_one[:, 1], ALU.add)
-                nc.sync.dma_start(out[cb * P : (cb + 1) * P, atoms], out_sb[:, atoms])
+                nc.scalar.copy(filt[:, i * PIECE : (i + 1) * PIECE], filt_ps[:])
+            prods[u] = ring.tile([P, GROUP * PIECE], F32, name="prod")
+            nc.vector.tensor_tensor(
+                prods[u][:],
+                xj[cb][:].indirect(offsets[:, g * (GROUP * PIECE // 16) : (g + 1) * (GROUP * PIECE // 16)]),
+                filt[:],
+                ALU.mult,
+            )
+
+        def add_pairs(u):
+            by_two = prods[u][:].rearrange("p (a m n) -> p m a n", m=2, n=2)
+            pair_sums[u] = ring.tile([P, GROUP * PIECE // 2], F32, name="pair_sum")
+            nc.vector.tensor_tensor(
+                pair_sums[u][:].rearrange("p (a n) -> p a n", n=2), by_two[:, 0], by_two[:, 1], ALU.add
+            )
+
+        def add_and_store(u):
+            cb, g = units[u]
+            atoms = slice(g * GROUP * ATOMS, (g + 1) * GROUP * ATOMS)
+            by_one = pair_sums[u][:].rearrange("p (a n) -> p n a", n=2)
+            nc.vector.tensor_tensor(out_sb[cb][:, atoms], by_one[:, 0], by_one[:, 1], ALU.add)
+            nc.sync.dma_start(out[cb * P : (cb + 1) * P, atoms], out_sb[cb][:, atoms])
+
+        for u in range(len(units) + 2):
+            if u < len(units):
+                look_up(u)
+            if 1 <= u <= len(units):
+                add_pairs(u - 1)
+            if u >= 2:
+                add_and_store(u - 2)

@@ -29,17 +29,12 @@ def tile_physnetinteraction_kernel(tc, x, dw, db, rbf, filt_w, dist, offs, out):
     ):
         dist_sb = held.tile([P, N // P], F32, name="dist_sb")
         nc.sync.dma_start(dist_sb[:], dist.rearrange("o (p i) -> (o p) i", p=P))
-        x_sb = held.tile([P, BLOCKS, S], F32, name="x_sb")
-        x_blocks = x.rearrange("(kb p) s -> p kb s", p=P)
-        for h in range(S // HALF):
-            cols = slice(h * HALF, (h + 1) * HALF)
-            nc.sync.dma_start(x_sb[:, :, cols], x_blocks[:, :, cols])
-        rbf_sb = held.tile([RB, N], BF16, name="rbf_sb")
-        for h in range(2):
-            cols = slice(h * (N // 2), (h + 1) * (N // 2))
-            nc.sync.dma_start(rbf_sb[:, cols], rbf[:, cols])
         offsets = held.tile([P, N // 16], U16, name="offsets")
         nc.sync.dma_start(offsets[:], offs)
+        x_sb = held.tile([P, BLOCKS, S], F32, name="x_sb")
+        nc.scalar.dma_start(x_sb[:], x.rearrange("(kb p) s -> p kb s", p=P))
+        rbf_sb = held.tile([RB, N], BF16, name="rbf_sb")
+        nc.scalar.dma_start(rbf_sb[:], rbf)
 
         dw_sb = held.tile([P, BLOCKS, C], BF16, name="dw_sb")
         nc.gpsimd.dma_start(dw_sb[:], dw.rearrange("(kb p) c -> p kb c", p=P))
@@ -76,8 +71,8 @@ def tile_physnetinteraction_kernel(tc, x, dw, db, rbf, filt_w, dist, offs, out):
             pairs = slice(k * PIECE, (k + 1) * PIECE)
             nc.vector.tensor_tensor(rbf_cut[:, pairs], rbf_sb[:, pairs], cut_all[:, pairs], ALU.mult)
 
-        xj = [held.tile([P, S], F32, name=f"xj{cb}") for cb in range(BLOCKS)]
         for cb in range(BLOCKS):
+            xj = held.tile([P, S], F32, name=f"xj{cb}")
             for h in range(S // HALF):
                 cols = slice(h * HALF, (h + 1) * HALF)
                 xj_ps = psum.tile([P, HALF], F32, name="xj_ps")
@@ -89,53 +84,35 @@ def tile_physnetinteraction_kernel(tc, x, dw, db, rbf, filt_w, dist, offs, out):
                         start=(kb == 0),
                         stop=(kb == BLOCKS - 1),
                     )
-                nc.scalar.activation(xj[cb][:, cols], xj_ps[:], ACT.Identity, bias=db_sb[cb][:, 0:1])
+                nc.scalar.activation(xj[:, cols], xj_ps[:], ACT.Identity, bias=db_sb[cb][:, 0:1])
 
-        out_sb = [held.tile([P, S], F32, name=f"out_sb{cb}") for cb in range(BLOCKS)]
-        units = [(cb, g) for cb in range(BLOCKS) for g in range(PIECES // GROUP)]
-        prods = {}
-        pair_sums = {}
-
-        def look_up(u):
-            cb, g = units[u]
-            filt = ring.tile([P, GROUP * PIECE], F32, name="filt")
-            for i in range(GROUP):
-                k = g * GROUP + i
-                filt_ps = psum.tile([P, PIECE], F32, name="filt_ps", bufs=4)
-                nc.tensor.matmul(
-                    filt_ps[:],
-                    fw32[:, cb * P : (cb + 1) * P],
-                    rbf_cut[:, k * PIECE : (k + 1) * PIECE],
-                    start=True,
-                    stop=True,
+            out_sb = held.tile([P, S], F32, name=f"out_sb{cb}")
+            for g in range(PIECES // GROUP):
+                atoms = slice(g * GROUP * ATOMS, (g + 1) * GROUP * ATOMS)
+                filt = ring.tile([P, GROUP * PIECE], F32, name="filt")
+                for i in range(GROUP):
+                    k = g * GROUP + i
+                    filt_ps = psum.tile([P, PIECE], F32, name="filt_ps", bufs=4)
+                    nc.tensor.matmul(
+                        filt_ps[:],
+                        fw32[:, cb * P : (cb + 1) * P],
+                        rbf_cut[:, k * PIECE : (k + 1) * PIECE],
+                        start=True,
+                        stop=True,
+                    )
+                    nc.scalar.copy(filt[:, i * PIECE : (i + 1) * PIECE], filt_ps[:])
+                prod = ring.tile([P, GROUP * PIECE], F32, name="prod")
+                nc.vector.tensor_tensor(
+                    prod[:],
+                    xj[:].indirect(offsets[:, g * (GROUP * PIECE // 16) : (g + 1) * (GROUP * PIECE // 16)]),
+                    filt[:],
+                    ALU.mult,
                 )
-                nc.scalar.copy(filt[:, i * PIECE : (i + 1) * PIECE], filt_ps[:])
-            prods[u] = ring.tile([P, GROUP * PIECE], F32, name="prod")
-            nc.vector.tensor_tensor(
-                prods[u][:],
-                xj[cb][:].indirect(offsets[:, g * (GROUP * PIECE // 16) : (g + 1) * (GROUP * PIECE // 16)]),
-                filt[:],
-                ALU.mult,
-            )
-
-        def add_pairs(u):
-            by_two = prods[u][:].rearrange("p (a m n) -> p m a n", m=2, n=2)
-            pair_sums[u] = ring.tile([P, GROUP * PIECE // 2], F32, name="pair_sum")
-            nc.vector.tensor_tensor(
-                pair_sums[u][:].rearrange("p (a n) -> p a n", n=2), by_two[:, 0], by_two[:, 1], ALU.add
-            )
-
-        def add_and_store(u):
-            cb, g = units[u]
-            atoms = slice(g * GROUP * ATOMS, (g + 1) * GROUP * ATOMS)
-            by_one = pair_sums[u][:].rearrange("p (a n) -> p n a", n=2)
-            nc.vector.tensor_tensor(out_sb[cb][:, atoms], by_one[:, 0], by_one[:, 1], ALU.add)
-            nc.sync.dma_start(out[cb * P : (cb + 1) * P, atoms], out_sb[cb][:, atoms])
-
-        for u in range(len(units) + 2):
-            if u < len(units):
-                look_up(u)
-            if 1 <= u <= len(units):
-                add_pairs(u - 1)
-            if u >= 2:
-                add_and_store(u - 2)
+                by_two = prod[:].rearrange("p (a m n) -> p m a n", m=2, n=2)
+                pair_sum = ring.tile([P, GROUP * PIECE // 2], F32, name="pair_sum")
+                nc.vector.tensor_tensor(
+                    pair_sum[:].rearrange("p (a n) -> p a n", n=2), by_two[:, 0], by_two[:, 1], ALU.add
+                )
+                by_one = pair_sum[:].rearrange("p (a n) -> p n a", n=2)
+                nc.vector.tensor_tensor(out_sb[:, atoms], by_one[:, 0], by_one[:, 1], ALU.add)
+                nc.sync.dma_start(out[cb * P : (cb + 1) * P, atoms], out_sb[:, atoms])

@@ -1,4 +1,5 @@
 import concourse.mybir as mybir
+from concourse.masks import make_identity
 
 F32 = mybir.dt.float32
 BF16 = mybir.dt.bfloat16
@@ -15,6 +16,7 @@ PIECE = 512
 PIECES = N // PIECE
 ATOMS = PIECE // NB
 GROUP = 2
+GROUPS = PIECES // GROUP
 PARK_ROWS = N // S
 
 FLOPS = 2 * C * C * S + 2 * RB * C * N
@@ -71,8 +73,11 @@ def tile_physnetinteraction_kernel(tc, x, dw, db, rbf, filt_w, dist, offs, out):
             pairs = slice(k * PIECE, (k + 1) * PIECE)
             nc.vector.tensor_tensor(rbf_cut[:, pairs], rbf_sb[:, pairs], cut_all[:, pairs], ALU.mult)
 
+        ident = held.tile([P, P], F32, name="ident")
+        make_identity(nc, ident[:])
+
+        xj = [held.tile([P, S], F32, name=f"xj{cb}") for cb in range(BLOCKS)]
         for cb in range(BLOCKS):
-            xj = held.tile([P, S], F32, name=f"xj{cb}")
             for h in range(S // HALF):
                 cols = slice(h * HALF, (h + 1) * HALF)
                 xj_ps = psum.tile([P, HALF], F32, name="xj_ps")
@@ -84,12 +89,11 @@ def tile_physnetinteraction_kernel(tc, x, dw, db, rbf, filt_w, dist, offs, out):
                         start=(kb == 0),
                         stop=(kb == BLOCKS - 1),
                     )
-                nc.scalar.activation(xj[:, cols], xj_ps[:], ACT.Identity, bias=db_sb[cb][:, 0:1])
+                nc.scalar.activation(xj[cb][:, cols], xj_ps[:], ACT.Identity, bias=db_sb[cb][:, 0:1])
 
-            out_sb = held.tile([P, S], F32, name=f"out_sb{cb}")
-            for g in range(PIECES // GROUP):
-                atoms = slice(g * GROUP * ATOMS, (g + 1) * GROUP * ATOMS)
-                filt = ring.tile([P, GROUP * PIECE], F32, name="filt")
+        filt = [[held.tile([P, GROUP * PIECE], F32, name=f"filt{cb}_{g}") for g in range(GROUPS)] for cb in range(BLOCKS)]
+        for cb in range(BLOCKS):
+            for g in range(GROUPS):
                 for i in range(GROUP):
                     k = g * GROUP + i
                     filt_ps = psum.tile([P, PIECE], F32, name="filt_ps", bufs=4)
@@ -100,19 +104,31 @@ def tile_physnetinteraction_kernel(tc, x, dw, db, rbf, filt_w, dist, offs, out):
                         start=True,
                         stop=True,
                     )
-                    nc.scalar.copy(filt[:, i * PIECE : (i + 1) * PIECE], filt_ps[:])
+                    nc.scalar.copy(filt[cb][g][:, i * PIECE : (i + 1) * PIECE], filt_ps[:])
+
+        for cb in range(BLOCKS):
+            out_sb = held.tile([P, S], F32, name=f"out_sb{cb}")
+            for g in range(GROUPS):
+                atoms = slice(g * GROUP * ATOMS, (g + 1) * GROUP * ATOMS)
                 prod = ring.tile([P, GROUP * PIECE], F32, name="prod")
                 nc.vector.tensor_tensor(
                     prod[:],
-                    xj[:].indirect(offsets[:, g * (GROUP * PIECE // 16) : (g + 1) * (GROUP * PIECE // 16)]),
-                    filt[:],
+                    xj[cb][:].indirect(offsets[:, g * (GROUP * PIECE // 16) : (g + 1) * (GROUP * PIECE // 16)]),
+                    filt[cb][g][:],
                     ALU.mult,
                 )
-                by_two = prod[:].rearrange("p (a m n) -> p m a n", m=2, n=2)
-                pair_sum = ring.tile([P, GROUP * PIECE // 2], F32, name="pair_sum")
-                nc.vector.tensor_tensor(
-                    pair_sum[:].rearrange("p (a n) -> p a n", n=2), by_two[:, 0], by_two[:, 1], ALU.add
-                )
-                by_one = pair_sum[:].rearrange("p (a n) -> p n a", n=2)
-                nc.vector.tensor_tensor(out_sb[:, atoms], by_one[:, 0], by_one[:, 1], ALU.add)
+                if cb == BLOCKS - 1 and g < GROUPS - 1:
+                    by_neighbour = prod[:].rearrange("p (a n) -> p n a", n=NB)
+                    sum_ps = psum.tile([P, GROUP * ATOMS], F32, name="sum_ps")
+                    for n in range(NB):
+                        nc.tensor.matmul(sum_ps[:], ident[:], by_neighbour[:, n], start=(n == 0), stop=(n == NB - 1))
+                    nc.scalar.copy(out_sb[:, atoms], sum_ps[:])
+                else:
+                    by_two = prod[:].rearrange("p (a m n) -> p m a n", m=2, n=2)
+                    pair_sum = ring.tile([P, GROUP * PIECE // 2], F32, name="pair_sum")
+                    nc.vector.tensor_tensor(
+                        pair_sum[:].rearrange("p (a n) -> p a n", n=2), by_two[:, 0], by_two[:, 1], ALU.add
+                    )
+                    by_one = pair_sum[:].rearrange("p (a n) -> p n a", n=2)
+                    nc.vector.tensor_tensor(out_sb[:, atoms], by_one[:, 0], by_one[:, 1], ALU.add)
                 nc.sync.dma_start(out[cb * P : (cb + 1) * P, atoms], out_sb[:, atoms])

@@ -12,12 +12,14 @@ C, S, NB, RB, N = 256, 1024, 4, 128, 4096
 CUTOFF = 5.0
 BLOCKS = C // P
 HALF = 512
+STRIPS = N // P
 PIECE = 512
-PIECES = N // PIECE
-ATOMS = PIECE // NB
-GROUP = 2
-GROUPS = PIECES // GROUP
-PARK_ROWS = N // S
+PIECE_STRIPS = PIECE // P
+LOOKUP = 1024
+GROUPS = N // LOOKUP
+GROUP_STRIPS = LOOKUP // P
+ATOMS = LOOKUP // NB
+FLIP_LAG = 2
 
 FLOPS = 2 * C * C * S + 2 * RB * C * N
 
@@ -27,60 +29,91 @@ def tile_physnetinteraction_kernel(tc, x, dw, db, rbf, filt_w, dist, offs, out):
     with (
         tc.tile_pool(name="held", bufs=1) as held,
         tc.tile_pool(name="ring", bufs=4) as ring,
-        tc.psum_pool(name="psum", bufs=2) as psum,
+        tc.psum_pool(name="psum", bufs=1) as psum,
     ):
-        dist_sb = held.tile([P, N // P], F32, name="dist_sb")
-        nc.sync.dma_start(dist_sb[:], dist.rearrange("o (p i) -> (o p) i", p=P))
+        ident = held.tile([P, P], F32, name="ident")
+        make_identity(nc, ident[:])
+
+        dist_rows = held.tile([2 * STRIPS, P], F32, name="dist_rows")
+        nc.vector.memset(dist_rows[STRIPS : 2 * STRIPS, :], 0.0)
+        nc.sync.dma_start(dist_rows[0:STRIPS, :], dist.rearrange("o (b p) -> (o b) p", p=P))
+        fw_sb = held.tile([RB, C], BF16, name="fw_sb")
+        nc.sync.dma_start(fw_sb[:], filt_w)
+        rbf_sb = held.tile([RB, N], BF16, name="rbf_sb")
+        nc.sync.dma_start(rbf_sb[:, 0:LOOKUP], rbf[:, 0:LOOKUP])
+        x_sb = held.tile([P, BLOCKS, S], F32, name="x_sb")
+        x_blocks = x.rearrange("(kb p) s -> p kb s", p=P)
+        for h in range(S // HALF):
+            cols = slice(h * HALF, (h + 1) * HALF)
+            nc.sync.dma_start(x_sb[:, :, cols], x_blocks[:, :, cols])
+        db_sb = held.tile([P, BLOCKS], F32, name="db_sb")
+        nc.sync.dma_start(db_sb[:], db.rearrange("(cb p) o -> p (cb o)", p=P))
         offsets = held.tile([P, N // 16], U16, name="offsets")
         nc.sync.dma_start(offsets[:], offs)
-        x_sb = held.tile([P, BLOCKS, S], F32, name="x_sb")
-        nc.scalar.dma_start(x_sb[:], x.rearrange("(kb p) s -> p kb s", p=P))
-        rbf_sb = held.tile([RB, N], BF16, name="rbf_sb")
-        nc.scalar.dma_start(rbf_sb[:], rbf)
-
         dw_sb = held.tile([P, BLOCKS, C], BF16, name="dw_sb")
         nc.gpsimd.dma_start(dw_sb[:], dw.rearrange("(kb p) c -> p kb c", p=P))
-        db_sb = [held.tile([P, 1], F32, name=f"db_sb{cb}") for cb in range(BLOCKS)]
-        for cb in range(BLOCKS):
-            nc.gpsimd.dma_start(db_sb[cb][:], db[cb * P : (cb + 1) * P, :])
-        fw_sb = held.tile([RB, C], BF16, name="fw_sb")
-        nc.gpsimd.dma_start(fw_sb[:], filt_w)
+        nc.gpsimd.dma_start(rbf_sb[:, LOOKUP:N], rbf[:, LOOKUP:N])
 
-        d2 = held.tile([P, N // P], F32, name="d2")
+        dist_ps = psum.tile([P, 2 * STRIPS], F32, name="dist_ps", tag="strip", bufs=3)
+        nc.tensor.transpose(dist_ps[:], dist_rows[:], ident[0 : 2 * STRIPS, 0 : 2 * STRIPS])
+        dist_sb = held.tile([P, STRIPS], F32, name="dist_sb")
+        nc.vector.tensor_copy(dist_sb[:], dist_ps[:, 0:STRIPS])
+        d2 = held.tile([P, STRIPS], F32, name="d2")
         nc.vector.tensor_tensor(d2[:], dist_sb[:], dist_sb[:], ALU.mult)
-        one_minus = held.tile([P, N // P], F32, name="one_minus")
+        one_minus = held.tile([P, STRIPS], F32, name="one_minus")
         nc.vector.tensor_scalar(one_minus[:], d2[:], -1.0 / (CUTOFF * CUTOFF), 1.0, ALU.mult, ALU.add)
-        recip = held.tile([P, N // P], F32, name="recip")
+        recip = held.tile([P, STRIPS], F32, name="recip")
         nc.vector.reciprocal(recip[:], one_minus[:])
-        cut = held.tile([P, N // P], F32, name="cut")
+        cut = held.tile([P, STRIPS], F32, name="cut")
         nc.scalar.activation(cut[:], recip[:], ACT.Exp, bias=1.0, scale=-1.0)
-
-        nc.sync.dma_start(out[0:PARK_ROWS, :].rearrange("r (q i) -> (r q) i", i=N // P), cut[:])
-        parked = out[0:PARK_ROWS, :].rearrange("r (h j) -> (r h) j", j=PIECE)
-        cut_all = held.tile([P, N], F32, name="cut_all")
-        for k in range(PIECES):
-            nc.sync.dma_start(cut_all[:, k * PIECE : (k + 1) * PIECE], parked[k : k + 1, :].broadcast_to([P, PIECE]))
 
         sw = held.tile([P, BLOCKS, S], BF16, name="sw")
         for h in range(S // HALF):
             for kb in range(BLOCKS):
                 cols = slice(h * HALF, (h + 1) * HALF)
                 nc.scalar.activation(sw[:, kb, cols], x_sb[:, kb, cols], ACT.Silu)
-        fw32 = held.tile([RB, C], F32, name="fw32")
-        nc.gpsimd.tensor_copy(fw32[:], fw_sb[:])
-        rbf_cut = held.tile([RB, N], F32, name="rbf_cut")
-        for k in range(PIECES):
-            pairs = slice(k * PIECE, (k + 1) * PIECE)
-            nc.vector.tensor_tensor(rbf_cut[:, pairs], rbf_sb[:, pairs], cut_all[:, pairs], ALU.mult)
 
-        ident = held.tile([P, P], F32, name="ident")
-        make_identity(nc, ident[:])
+        filt = [[held.tile([P, LOOKUP], F32, name=f"filt{cb}_{g}") for g in range(GROUPS)] for cb in range(BLOCKS)]
+
+        def flip_strips(g):
+            scaled = {}
+            banks = {}
+            for step in range(GROUP_STRIPS + FLIP_LAG):
+                if step < GROUP_STRIPS:
+                    b = g * GROUP_STRIPS + step
+                    strip_ps = psum.tile([P, C], F32, name="strip_ps", tag="strip", bufs=3)
+                    nc.tensor.matmul(strip_ps[:], rbf_sb[:, b * P : (b + 1) * P], fw_sb[:], start=True, stop=True)
+                    scaled[step] = ring.tile([P, C], F32, name="scaled")
+                    if g == 0:
+                        nc.vector.tensor_scalar(scaled[step][:], strip_ps[:], cut[:, b : b + 1], None, ALU.mult)
+                    else:
+                        nc.scalar.activation(scaled[step][:], strip_ps[:], ACT.Identity, scale=cut[:, b : b + 1])
+                if step >= FLIP_LAG:
+                    i, q = divmod(step - FLIP_LAG, PIECE_STRIPS)
+                    for cb in range(BLOCKS):
+                        if q == 0:
+                            banks[cb, i] = psum.tile([P, PIECE], F32, name=f"filt_ps{cb}", tag="bank", bufs=5)
+                        nc.tensor.transpose(
+                            banks[cb, i][:, q * P : (q + 1) * P],
+                            scaled[step - FLIP_LAG][:, cb * P : (cb + 1) * P],
+                            ident[:],
+                        )
+            return banks
+
+        def bring_out(g, cb, banks):
+            for i in range(LOOKUP // PIECE):
+                target = filt[cb][g][:, i * PIECE : (i + 1) * PIECE]
+                if g == 0 and cb == 0:
+                    nc.vector.tensor_copy(target, banks[cb, i][:])
+                else:
+                    nc.scalar.copy(target, banks[cb, i][:])
 
         xj = [held.tile([P, S], F32, name=f"xj{cb}") for cb in range(BLOCKS)]
-        for cb in range(BLOCKS):
+
+        def make_window(cb):
             for h in range(S // HALF):
                 cols = slice(h * HALF, (h + 1) * HALF)
-                xj_ps = psum.tile([P, HALF], F32, name="xj_ps")
+                xj_ps = psum.tile([P, HALF], F32, name="xj_ps", tag="bank", bufs=5)
                 for kb in range(BLOCKS):
                     nc.tensor.matmul(
                         xj_ps[:],
@@ -89,46 +122,33 @@ def tile_physnetinteraction_kernel(tc, x, dw, db, rbf, filt_w, dist, offs, out):
                         start=(kb == 0),
                         stop=(kb == BLOCKS - 1),
                     )
-                nc.scalar.activation(xj[cb][:, cols], xj_ps[:], ACT.Identity, bias=db_sb[cb][:, 0:1])
+                nc.scalar.activation(xj[cb][:, cols], xj_ps[:], ACT.Identity, bias=db_sb[:, cb : cb + 1])
 
-        filt = [[held.tile([P, GROUP * PIECE], F32, name=f"filt{cb}_{g}") for g in range(GROUPS)] for cb in range(BLOCKS)]
+        banks = flip_strips(0)
         for cb in range(BLOCKS):
-            for g in range(GROUPS):
-                for i in range(GROUP):
-                    k = g * GROUP + i
-                    filt_ps = psum.tile([P, PIECE], F32, name="filt_ps", bufs=4)
-                    nc.tensor.matmul(
-                        filt_ps[:],
-                        fw32[:, cb * P : (cb + 1) * P],
-                        rbf_cut[:, k * PIECE : (k + 1) * PIECE],
-                        start=True,
-                        stop=True,
-                    )
-                    nc.scalar.copy(filt[cb][g][:, i * PIECE : (i + 1) * PIECE], filt_ps[:])
+            make_window(cb)
+            bring_out(0, cb, banks)
 
-        for cb in range(BLOCKS):
-            out_sb = held.tile([P, S], F32, name=f"out_sb{cb}")
-            for g in range(GROUPS):
-                atoms = slice(g * GROUP * ATOMS, (g + 1) * GROUP * ATOMS)
-                prod = ring.tile([P, GROUP * PIECE], F32, name="prod")
+        out_sb = [held.tile([P, S], F32, name=f"out_sb{cb}") for cb in range(BLOCKS)]
+        for g in range(GROUPS):
+            if g + 1 < GROUPS:
+                banks = flip_strips(g + 1)
+                for cb in range(BLOCKS):
+                    bring_out(g + 1, cb, banks)
+            atoms = slice(g * ATOMS, (g + 1) * ATOMS)
+            for cb in range(BLOCKS):
+                prod = ring.tile([P, LOOKUP], F32, name="prod")
                 nc.vector.tensor_tensor(
                     prod[:],
-                    xj[cb][:].indirect(offsets[:, g * (GROUP * PIECE // 16) : (g + 1) * (GROUP * PIECE // 16)]),
+                    xj[cb][:].indirect(offsets[:, g * (LOOKUP // 16) : (g + 1) * (LOOKUP // 16)]),
                     filt[cb][g][:],
                     ALU.mult,
                 )
-                if cb == BLOCKS - 1 and g < GROUPS - 1:
-                    by_neighbour = prod[:].rearrange("p (a n) -> p n a", n=NB)
-                    sum_ps = psum.tile([P, GROUP * ATOMS], F32, name="sum_ps")
-                    for n in range(NB):
-                        nc.tensor.matmul(sum_ps[:], ident[:], by_neighbour[:, n], start=(n == 0), stop=(n == NB - 1))
-                    nc.scalar.copy(out_sb[:, atoms], sum_ps[:])
-                else:
-                    by_two = prod[:].rearrange("p (a m n) -> p m a n", m=2, n=2)
-                    pair_sum = ring.tile([P, GROUP * PIECE // 2], F32, name="pair_sum")
-                    nc.vector.tensor_tensor(
-                        pair_sum[:].rearrange("p (a n) -> p a n", n=2), by_two[:, 0], by_two[:, 1], ALU.add
-                    )
-                    by_one = pair_sum[:].rearrange("p (a n) -> p n a", n=2)
-                    nc.vector.tensor_tensor(out_sb[:, atoms], by_one[:, 0], by_one[:, 1], ALU.add)
-                nc.sync.dma_start(out[cb * P : (cb + 1) * P, atoms], out_sb[:, atoms])
+                by_two = prod[:].rearrange("p (a m n) -> p m a n", m=2, n=2)
+                pair_sum = ring.tile([P, LOOKUP // 2], F32, name="pair_sum")
+                nc.vector.tensor_tensor(
+                    pair_sum[:].rearrange("p (a n) -> p a n", n=2), by_two[:, 0], by_two[:, 1], ALU.add
+                )
+                by_one = pair_sum[:].rearrange("p (a n) -> p n a", n=2)
+                nc.vector.tensor_tensor(out_sb[cb][:, atoms], by_one[:, 0], by_one[:, 1], ALU.add)
+                nc.sync.dma_start(out[cb * P : (cb + 1) * P, atoms], out_sb[cb][:, atoms])

@@ -37,15 +37,15 @@ def tile_physnetinteraction_kernel(tc, x, dw, db, rbf, filt_w, dist, offs, out):
         dist_rows = held.tile([2 * STRIPS, P], F32, name="dist_rows")
         nc.vector.memset(dist_rows[STRIPS : 2 * STRIPS, :], 0.0)
         nc.sync.dma_start(dist_rows[0:STRIPS, :], dist.rearrange("o (b p) -> (o b) p", p=P))
-        fw_sb = held.tile([RB, C], BF16, name="fw_sb")
-        nc.sync.dma_start(fw_sb[:], filt_w)
-        rbf_sb = held.tile([RB, N], BF16, name="rbf_sb")
-        nc.sync.dma_start(rbf_sb[:, 0:LOOKUP], rbf[:, 0:LOOKUP])
         x_sb = held.tile([P, BLOCKS, S], F32, name="x_sb")
         x_blocks = x.rearrange("(kb p) s -> p kb s", p=P)
         for h in range(S // HALF):
             cols = slice(h * HALF, (h + 1) * HALF)
             nc.sync.dma_start(x_sb[:, :, cols], x_blocks[:, :, cols])
+        rbf_sb = held.tile([RB, N], BF16, name="rbf_sb")
+        nc.sync.dma_start(rbf_sb[:, 0:LOOKUP], rbf[:, 0:LOOKUP])
+        fw_sb = held.tile([RB, C], BF16, name="fw_sb")
+        nc.sync.dma_start(fw_sb[:], filt_w)
         db_sb = held.tile([P, BLOCKS], F32, name="db_sb")
         nc.sync.dma_start(db_sb[:], db.rearrange("(cb p) o -> p (cb o)", p=P))
         offsets = held.tile([P, N // 16], U16, name="offsets")

@@ -37,15 +37,15 @@ def tile_physnetinteraction_kernel(tc, x, dw, db, rbf, filt_w, dist, offs, out):
         dist_rows = held.tile([2 * STRIPS, P], F32, name="dist_rows")
         nc.vector.memset(dist_rows[STRIPS : 2 * STRIPS, :], 0.0)
         nc.sync.dma_start(dist_rows[0:STRIPS, :], dist.rearrange("o (b p) -> (o b) p", p=P))
+        rbf_sb = held.tile([RB, N], BF16, name="rbf_sb")
+        nc.sync.dma_start(rbf_sb[:, 0:LOOKUP], rbf[:, 0:LOOKUP])
+        fw_sb = held.tile([RB, C], BF16, name="fw_sb")
+        nc.sync.dma_start(fw_sb[:], filt_w)
         x_sb = held.tile([P, BLOCKS, S], F32, name="x_sb")
         x_blocks = x.rearrange("(kb p) s -> p kb s", p=P)
         for h in range(S // HALF):
             cols = slice(h * HALF, (h + 1) * HALF)
             nc.sync.dma_start(x_sb[:, :, cols], x_blocks[:, :, cols])
-        rbf_sb = held.tile([RB, N], BF16, name="rbf_sb")
-        nc.sync.dma_start(rbf_sb[:, 0:LOOKUP], rbf[:, 0:LOOKUP])
-        fw_sb = held.tile([RB, C], BF16, name="fw_sb")
-        nc.sync.dma_start(fw_sb[:], filt_w)
         db_sb = held.tile([P, BLOCKS], F32, name="db_sb")
         nc.sync.dma_start(db_sb[:], db.rearrange("(cb p) o -> p (cb o)", p=P))
         offsets = held.tile([P, N // 16], U16, name="offsets")
@@ -62,12 +62,12 @@ def tile_physnetinteraction_kernel(tc, x, dw, db, rbf, filt_w, dist, offs, out):
         nc.vector.tensor_tensor(d2[:], dist_sb[:], dist_sb[:], ALU.mult)
         one_minus = held.tile([P, STRIPS], F32, name="one_minus")
         nc.vector.tensor_scalar(one_minus[:], d2[:], -1.0 / (CUTOFF * CUTOFF), 1.0, ALU.mult, ALU.add)
-        recip = held.tile([P, STRIPS], F32, name="recip")
+        recip = held.tile([P, STRIPS], F32, name="recip", tag="exp_then_swish")
         nc.vector.reciprocal(recip[:], one_minus[:])
         cut = held.tile([P, STRIPS], F32, name="cut")
         nc.scalar.activation(cut[:], recip[:], ACT.Exp, bias=1.0, scale=-1.0)
 
-        sw = held.tile([P, BLOCKS, S], BF16, name="sw")
+        sw = held.tile([P, BLOCKS, S], BF16, name="sw", tag="exp_then_swish")
         for h in range(S // HALF):
             for kb in range(BLOCKS):
                 cols = slice(h * HALF, (h + 1) * HALF)

@@ -41,6 +41,8 @@ def tile_physnetinteraction_kernel(tc, x, dw, db, rbf, filt_w, dist, offs, out):
         nc.sync.dma_start(rbf_sb[:, 0:LOOKUP], rbf[:, 0:LOOKUP])
         fw_sb = held.tile([RB, C], BF16, name="fw_sb")
         nc.sync.dma_start(fw_sb[:], filt_w)
+        dw_sb = held.tile([P, BLOCKS, C], BF16, name="dw_sb")
+        nc.sync.dma_start(dw_sb[:], dw.rearrange("(kb p) c -> p kb c", p=P))
         x_sb = held.tile([P, BLOCKS, S], F32, name="x_sb")
         x_blocks = x.rearrange("(kb p) s -> p kb s", p=P)
         for h in range(S // HALF):
@@ -50,8 +52,6 @@ def tile_physnetinteraction_kernel(tc, x, dw, db, rbf, filt_w, dist, offs, out):
         nc.sync.dma_start(db_sb[:], db.rearrange("(cb p) o -> p (cb o)", p=P))
         offsets = held.tile([P, N // 16], U16, name="offsets")
         nc.sync.dma_start(offsets[:], offs)
-        dw_sb = held.tile([P, BLOCKS, C], BF16, name="dw_sb")
-        nc.gpsimd.dma_start(dw_sb[:], dw.rearrange("(kb p) c -> p kb c", p=P))
         nc.gpsimd.dma_start(rbf_sb[:, LOOKUP:N], rbf[:, LOOKUP:N])
 
         dist_ps = psum.tile([P, 2 * STRIPS], F32, name="dist_ps", tag="strip", bufs=3)

@@ -52,7 +52,7 @@ def tile_physnetinteraction_kernel(tc, x, dw, db, rbf, filt_w, dist, offs, out):
         nc.sync.dma_start(db_sb[:], db.rearrange("(cb p) o -> p (cb o)", p=P))
         offsets = held.tile([P, N // 16], U16, name="offsets")
         nc.sync.dma_start(offsets[:], offs)
-        nc.gpsimd.dma_start(rbf_sb[:, LOOKUP:N], rbf[:, LOOKUP:N])
+        nc.sync.dma_start(rbf_sb[:, LOOKUP:N], rbf[:, LOOKUP:N])
 
         dist_ps = psum.tile([P, 2 * STRIPS], F32, name="dist_ps", tag="strip", bufs=3)
         nc.tensor.transpose(dist_ps[:], dist_rows[:], ident[0 : 2 * STRIPS, 0 : 2 * STRIPS])

import concourse.mybir as mybir
from concourse.masks import make_identity

F32 = mybir.dt.float32
BF16 = mybir.dt.bfloat16
U16 = mybir.dt.uint16
ACT = mybir.ActivationFunctionType
ALU = mybir.AluOpType

P = 128
C, S, NB, RB, N = 256, 1024, 4, 128, 4096
CUTOFF = 5.0
BLOCKS = C // P
HALF = 512
STRIPS = N // P
PIECE = 512
PIECE_STRIPS = PIECE // P
LOOKUP = 1024
GROUPS = N // LOOKUP
GROUP_STRIPS = LOOKUP // P
ATOMS = LOOKUP // NB
FLIP_LAG = 2

FLOPS = 2 * C * C * S + 2 * RB * C * N


def tile_physnetinteraction_kernel(tc, x, dw, db, rbf, filt_w, dist, offs, out):
    nc = tc.nc
    with (
        tc.tile_pool(name="held", bufs=1) as held,
        tc.tile_pool(name="ring", bufs=4) as ring,
        tc.psum_pool(name="psum", bufs=1) as psum,
    ):
        ident = held.tile([P, P], F32, name="ident")
        make_identity(nc, ident[:])

        dist_rows = held.tile([2 * STRIPS, P], F32, name="dist_rows")
        nc.vector.memset(dist_rows[STRIPS : 2 * STRIPS, :], 0.0)
        nc.sync.dma_start(dist_rows[0:STRIPS, :], dist.rearrange("o (b p) -> (o b) p", p=P))
        rbf_sb = held.tile([RB, N], BF16, name="rbf_sb")
        nc.sync.dma_start(rbf_sb[:, 0:LOOKUP], rbf[:, 0:LOOKUP])
        fw_sb = held.tile([RB, C], BF16, name="fw_sb")
        nc.sync.dma_start(fw_sb[:], filt_w)
        dw_sb = held.tile([P, BLOCKS, C], BF16, name="dw_sb")
        nc.sync.dma_start(dw_sb[:], dw.rearrange("(kb p) c -> p kb c", p=P))
        x_sb = held.tile([P, BLOCKS, S], F32, name="x_sb")
        x_blocks = x.rearrange("(kb p) s -> p kb s", p=P)
        for h in range(S // HALF):
            cols = slice(h * HALF, (h + 1) * HALF)
            nc.sync.dma_start(x_sb[:, :, cols], x_blocks[:, :, cols])
        db_sb = held.tile([P, BLOCKS], F32, name="db_sb")
        nc.sync.dma_start(db_sb[:], db.rearrange("(cb p) o -> p (cb o)", p=P))
        offsets = held.tile([P, N // 16], U16, name="offsets")
        nc.sync.dma_start(offsets[:], offs)
        nc.sync.dma_start(rbf_sb[:, LOOKUP:N], rbf[:, LOOKUP:N])

        dist_ps = psum.tile([P, 2 * STRIPS], F32, name="dist_ps", tag="strip", bufs=3)
        nc.tensor.transpose(dist_ps[:], dist_rows[:], ident[0 : 2 * STRIPS, 0 : 2 * STRIPS])
        dist_sb = held.tile([P, STRIPS], F32, name="dist_sb")
        nc.vector.tensor_copy(dist_sb[:], dist_ps[:, 0:STRIPS])
        d2 = held.tile([P, STRIPS], F32, name="d2")
        nc.vector.tensor_tensor(d2[:], dist_sb[:], dist_sb[:], ALU.mult)
        one_minus = held.tile([P, STRIPS], F32, name="one_minus")
        nc.vector.tensor_scalar(one_minus[:], d2[:], -1.0 / (CUTOFF * CUTOFF), 1.0, ALU.mult, ALU.add)
        recip = held.tile([P, STRIPS], F32, name="recip", tag="exp_then_swish")
        nc.vector.reciprocal(recip[:], one_minus[:])
        cut = held.tile([P, STRIPS], F32, name="cut")
        nc.scalar.activation(cut[:], recip[:], ACT.Exp, bias=1.0, scale=-1.0)

        sw = held.tile([P, BLOCKS, S], BF16, name="sw", tag="exp_then_swish")
        for h in range(S // HALF):
            for kb in range(BLOCKS):
                cols = slice(h * HALF, (h + 1) * HALF)
                nc.scalar.activation(sw[:, kb, cols], x_sb[:, kb, cols], ACT.Silu)

        filt = [[held.tile([P, LOOKUP], F32, name=f"filt{cb}_{g}") for g in range(GROUPS)] for cb in range(BLOCKS)]

        def flip_strips(g):
            scaled = {}
            banks = {}
            for step in range(GROUP_STRIPS + FLIP_LAG):
                if step < GROUP_STRIPS:
                    b = g * GROUP_STRIPS + step
                    strip_ps = psum.tile([P, C], F32, name="strip_ps", tag="strip", bufs=3)
                    nc.tensor.matmul(strip_ps[:], rbf_sb[:, b * P : (b + 1) * P], fw_sb[:], start=True, stop=True)
                    scaled[step] = ring.tile([P, C], F32, name="scaled")
                    if g == 0:
                        nc.vector.tensor_scalar(scaled[step][:], strip_ps[:], cut[:, b : b + 1], None, ALU.mult)
                    else:
                        nc.scalar.activation(scaled[step][:], strip_ps[:], ACT.Identity, scale=cut[:, b : b + 1])
                if step >= FLIP_LAG:
                    i, q = divmod(step - FLIP_LAG, PIECE_STRIPS)
                    for cb in range(BLOCKS):
                        if q == 0:
                            banks[cb, i] = psum.tile([P, PIECE], F32, name=f"filt_ps{cb}", tag="bank", bufs=5)
                        nc.tensor.transpose(
                            banks[cb, i][:, q * P : (q + 1) * P],
                            scaled[step - FLIP_LAG][:, cb * P : (cb + 1) * P],
                            ident[:],
                        )
            return banks

        def bring_out(g, cb, banks):
            for i in range(LOOKUP // PIECE):
                target = filt[cb][g][:, i * PIECE : (i + 1) * PIECE]
                if g == 0 and cb == 0:
                    nc.vector.tensor_copy(target, banks[cb, i][:])
                else:
                    nc.scalar.copy(target, banks[cb, i][:])

        xj = [held.tile([P, S], F32, name=f"xj{cb}") for cb in range(BLOCKS)]

        def make_window(cb):
            for h in range(S // HALF):
                cols = slice(h * HALF, (h + 1) * HALF)
                xj_ps = psum.tile([P, HALF], F32, name="xj_ps", tag="bank", bufs=5)
                for kb in range(BLOCKS):
                    nc.tensor.matmul(
                        xj_ps[:],
                        dw_sb[:, kb, cb * P : (cb + 1) * P],
                        sw[:, kb, cols],
                        start=(kb == 0),
                        stop=(kb == BLOCKS - 1),
                    )
                nc.scalar.activation(xj[cb][:, cols], xj_ps[:], ACT.Identity, bias=db_sb[:, cb : cb + 1])

        banks = flip_strips(0)
        for cb in range(BLOCKS):
            make_window(cb)
            bring_out(0, cb, banks)

        out_sb = [held.tile([P, S], F32, name=f"out_sb{cb}") for cb in range(BLOCKS)]
        for g in range(GROUPS):
            if g + 1 < GROUPS:
                banks = flip_strips(g + 1)
                for cb in range(BLOCKS):
                    bring_out(g + 1, cb, banks)
            atoms = slice(g * ATOMS, (g + 1) * ATOMS)
            for cb in range(BLOCKS):
                prod = ring.tile([P, LOOKUP], F32, name="prod")
                nc.vector.tensor_tensor(
                    prod[:],
                    xj[cb][:].indirect(offsets[:, g * (LOOKUP // 16) : (g + 1) * (LOOKUP // 16)]),
                    filt[cb][g][:],
                    ALU.mult,
                )
                by_two = prod[:].rearrange("p (a m n) -> p m a n", m=2, n=2)
                pair_sum = ring.tile([P, LOOKUP // 2], F32, name="pair_sum")
                nc.vector.tensor_tensor(
                    pair_sum[:].rearrange("p (a n) -> p a n", n=2), by_two[:, 0], by_two[:, 1], ALU.add
                )
                by_one = pair_sum[:].rearrange("p (a n) -> p n a", n=2)
                nc.vector.tensor_tensor(out_sb[cb][:, atoms], by_one[:, 0], by_one[:, 1], ALU.add)
                nc.sync.dma_start(out[cb * P : (cb + 1) * P, atoms], out_sb[cb][:, atoms])
